import numpy as np
import ml_dtypes


def mxq(x, axis, fmt="e4m3"):
    dtype, down = {"e4m3": (ml_dtypes.float8_e4m3fn, 7), "e5m2": (ml_dtypes.float8_e5m2, 14)}[fmt]
    v = np.moveaxis(np.asarray(x, np.float32).astype(ml_dtypes.bfloat16).astype(np.float64), axis, -1)
    blocks = v.reshape(v.shape[:-1] + (-1, 32))
    amax = np.abs(blocks).max(-1, keepdims=True)
    byte = np.maximum(np.where(amax > 0, np.frexp(amax)[1] - 1 + 127, 0) - down, 1)
    scale = np.exp2(byte - 127.0)
    codes = (blocks / scale).astype(np.float32).astype(dtype).astype(np.float64)
    return np.moveaxis((codes * scale).reshape(v.shape), -1, axis)


WIDE = False


def mx_kscale(k):
    if not WIDE:
        return np.ones(k)
    levels = np.array([10, -10, 5, -5, 0])
    a = np.random.permutation(np.resize(levels, k // 512 * 4)).reshape(k // 512, 4)
    idx = np.arange(k)
    return np.exp2(a[idx // 512, idx % 128 // 32])


BF16 = ml_dtypes.bfloat16


def bf(x):
    return np.asarray(x, np.float32).astype(BF16)


def f64(x):
    return np.asarray(x).astype(np.float64)


B, S, DIM, H, C, NOPE, ROPE, VDIM = 8, 1024, 512, 8, 128, 64, 128, 128
THETA = 10000.0
EPS = 1e-6


def rope_tables():
    freqs = 1.0 / THETA ** (np.arange(0, ROPE, 2, dtype=np.float64) / ROPE)
    ang = np.outer(np.arange(S, dtype=np.float64), freqs)
    return np.cos(ang), np.sin(ang)


def setup_inputs():
    s = mx_kscale(DIM)
    return {"x": bf(np.random.standard_normal((B, S, DIM)) * s),
            "wkv_a": bf(np.random.standard_normal((C + ROPE, DIM)) / np.sqrt(DIM) / s),
            "kv_norm_w": bf(1.0 + 0.1 * np.random.standard_normal(C))}


def reference(x, wkv_a, kv_norm_w):
    kv = mxq(f64(x), 2, "e4m3") @ mxq(f64(wkv_a), 1, "e4m3").T
    kv_lat, k_raw = kv[..., :C], kv[..., C:]
    cos, sin = rope_tables()
    x0, x1 = k_raw[..., 0::2], k_raw[..., 1::2]
    r0 = x0 * cos - x1 * sin
    r1 = x0 * sin + x1 * cos
    k_pe = np.stack([r0, r1], axis=-1).reshape(B, S, ROPE)
    rms = np.sqrt(np.mean(kv_lat * kv_lat, axis=-1, keepdims=True) + EPS)
    kv_cache = kv_lat / rms * f64(kv_norm_w)
    return kv_cache, k_pe

@@ -1,0 +1,222 @@
+import math
+from contextlib import ExitStack
+
+import concourse.mybir as mybir
+from concourse.masks import make_identity
+
+F32 = mybir.dt.float32
+BF16 = mybir.dt.bfloat16
+U32 = mybir.dt.uint32
+U8 = mybir.dt.uint8
+FP8X4 = mybir.dt.float8_e4m3fn_x4
+ALU = mybir.AluOpType
+ACT = mybir.ActivationFunctionType
+
+P = 128
+BATCH, SEQ, DIM = 8, 1024, 512
+LATENT, ROPE = 128, 128
+PAIRS = ROPE // 2
+DOUBLINGS = 6
+assert 2**DOUBLINGS == PAIRS
+THETA = 10000.0
+EPS = 1e-6
+
+WORDS = DIM // 2
+PER_PARTITION = SEQ // P
+TILES = 4
+HALVES = PER_PARTITION // TILES
+GROUPS = BATCH * HALVES
+
+ROUND = 1.5 * 2.0**23
+
+FLOPS = 2 * BATCH * SEQ * DIM * (LATENT + ROPE)
+
+
+def transpose_for_quantize(nc, psum_t, identity, rows, grouped, row_tiles):
+    row_words = rows[:].bitcast(F32)
+    grouped_words = grouped[:].bitcast(F32)
+    for pair in range(row_tiles // 2):
+        flipped = psum_t.tile([P, 2, 2, P], F32)
+        for t in range(2):
+            for u in range(2):
+                first = (2 * pair + t) * WORDS + u * P
+                nc.tensor.transpose(flipped[:, t, u, :], row_words[:, first : first + P], identity[:])
+        nc.scalar.copy(
+            out=grouped_words[:, 2 * pair * WORDS : 2 * (pair + 1) * WORDS].rearrange(
+                "p (t r u) -> p t r u", t=2, u=2
+            ),
+            in_=flipped[:].rearrange("p t u r -> p t r u"),
+        )
+
+
+def rotation_tables(nc, const):
+    position = const.tile([P, PER_PARTITION], F32)
+    nc.gpsimd.iota(
+        position[:],
+        pattern=[[1, PER_PARTITION]],
+        base=0,
+        channel_multiplier=PER_PARTITION,
+        allow_small_or_imprecise_dtypes=True,
+    )
+    turns = const.tile([P, 2, PER_PARTITION, PAIRS], F32)
+    nc.vector.tensor_scalar_mul(
+        out=turns[:, 0, :, 0:1], in0=position[:].unsqueeze(2), scalar1=1.0 / (2.0 * math.pi)
+    )
+    for doubling in range(DOUBLINGS):
+        width = 2**doubling
+        nc.vector.tensor_scalar_mul(
+            out=turns[:, 0, :, width : 2 * width],
+            in0=turns[:, 0, :, 0:width],
+            scalar1=THETA ** (-2.0 * width / ROPE),
+        )
+    nc.vector.tensor_scalar_add(out=turns[:, 1], in0=turns[:, 0], scalar1=0.25)
+    whole = const.tile([P, 2, PER_PARTITION, PAIRS], F32)
+    nc.vector.tensor_scalar(
+        out=whole[:], in0=turns[:], scalar1=ROUND, scalar2=ROUND, op0=ALU.add, op1=ALU.subtract
+    )
+    part = const.tile([P, 2, PER_PARTITION, PAIRS], F32)
+    nc.vector.tensor_tensor(out=part[:], in0=turns[:], in1=whole[:], op=ALU.subtract)
+    sin = const.tile([P, PER_PARTITION, PAIRS], F32)
+    neg_sin = const.tile([P, PER_PARTITION, PAIRS], F32)
+    cos = const.tile([P, PER_PARTITION, PAIRS], F32)
+    nc.scalar.activation(out=sin[:], in_=part[:, 0], func=ACT.Sin, scale=2.0 * math.pi)
+    nc.scalar.activation(out=neg_sin[:], in_=part[:, 0], func=ACT.Sin, scale=-2.0 * math.pi)
+    nc.scalar.activation(out=cos[:], in_=part[:, 1], func=ACT.Sin, scale=2.0 * math.pi)
+    return sin, neg_sin, cos
+
+
+def tile_simplemla_pa_t_kernel(tc, x, wkv_a, kv_norm_w, out_0, out_1):
+    nc = tc.nc
+    with ExitStack() as stack:
+        const = stack.enter_context(tc.tile_pool(name="const", bufs=1))
+        resident = stack.enter_context(tc.tile_pool(name="resident", bufs=GROUPS))
+        work = stack.enter_context(tc.tile_pool(name="work", bufs=3))
+        psum_t = stack.enter_context(tc.psum_pool(name="psum_t", bufs=4))
+        psum_kv = stack.enter_context(tc.psum_pool(name="psum_kv", bufs=2))
+
+        w_rows = const.tile([P, 2 * DIM], BF16)
+        nc.sync.dma_start(
+            out=w_rows[:].rearrange("p (a k) -> p a k", a=2),
+            in_=wkv_a.rearrange("(a p) k -> p a k", p=P),
+        )
+        gain = const.tile([P, LATENT], BF16)
+        nc.scalar.dma_start(out=gain[:], in_=kv_norm_w.partition_broadcast(P))
+        x_rows = []
+        for g in range(GROUPS):
+            b, half = divmod(g, HALVES)
+            x_group = resident.tile([P, TILES * DIM], BF16)
+            nc.sync.dma_start(
+                out=x_group[:].rearrange("p (i k) -> p i k", i=TILES),
+                in_=x[b].rearrange("(p i) k -> p i k", i=PER_PARTITION)[
+                    :, half * TILES : (half + 1) * TILES, :
+                ],
+            )
+            x_rows.append(x_group)
+
+        identity = const.tile([P, P], F32)
+        make_identity(nc, identity[:])
+        sin, neg_sin, cos = rotation_tables(nc, const)
+
+        w_grouped = const.tile([P, 2 * DIM], BF16, align_bytes=64)
+        transpose_for_quantize(nc, psum_t, identity, w_rows, w_grouped, 2)
+        w_codes = const.tile([P, 2 * P], U32, align_bytes=64)
+        w_scales = const.tile([P, 2 * P], U8, align_bytes=64)
+        nc.vector.quantize_mx(out=w_codes[:].bitcast(FP8X4), scales=w_scales[:], in_=w_grouped[:])
+
+        grouped_of = {}
+        kv_of = {}
+
+        def transpose_group(g):
+            x_grouped = work.tile([P, TILES * DIM], BF16, align_bytes=64)
+            transpose_for_quantize(nc, psum_t, identity, x_rows[g], x_grouped, TILES)
+            grouped_of[g] = x_grouped
+
+        def project_group(g):
+            x_codes = work.tile([P, TILES * P], U32, align_bytes=64)
+            x_scales = work.tile([P, TILES * P], U8, align_bytes=64)
+            nc.vector.quantize_mx(
+                out=x_codes[:].bitcast(FP8X4), scales=x_scales[:], in_=grouped_of[g][:]
+            )
+            latent = psum_kv.tile([P, TILES, LATENT], F32)
+            raw = psum_kv.tile([P, TILES, ROPE], F32)
+            for t in range(TILES):
+                tokens = slice(t * P, (t + 1) * P)
+                for result, columns in ((latent, slice(0, LATENT)), (raw, slice(LATENT, LATENT + ROPE))):
+                    nc.tensor.matmul_mx(
+                        out=result[:, t, :],
+                        lhsT=x_codes[:, tokens].bitcast(FP8X4),
+                        lhsT_scale=x_scales[:, tokens],
+                        rhs=w_codes[:, columns].bitcast(FP8X4),
+                        rhs_scale=w_scales[:, columns],
+                        start=True,
+                        stop=True,
+                    )
+            squares = work.tile([P, TILES, LATENT], F32)
+            sum_squares = work.tile([P, TILES], F32)
+            for t in range(TILES):
+                nc.scalar.activation(
+                    out=squares[:, t, :],
+                    in_=latent[:, t, :],
+                    func=ACT.Square,
+                    accum_out=sum_squares[:, t : t + 1],
+                )
+            rms = work.tile([P, TILES], F32)
+            nc.scalar.activation(
+                out=rms[:], in_=sum_squares[:], func=ACT.Sqrt, scale=1.0 / LATENT, bias=EPS
+            )
+            kv_of[g] = (latent, raw, rms)
+
+        def finish_group(g):
+            b, half = divmod(g, HALVES)
+            here = slice(half * TILES, (half + 1) * TILES)
+            latent, raw, rms = kv_of[g]
+            inv_rms = work.tile([P, TILES], F32)
+            nc.vector.reciprocal(out=inv_rms[:], in_=rms[:])
+
+            raw_pairs = raw[:].rearrange("p t (j e) -> p t j e", e=2)
+            direct = work.tile([P, TILES, PAIRS, 2], F32)
+            crossed = work.tile([P, 2, TILES, PAIRS], F32)
+            nc.vector.tensor_tensor(
+                out=direct[:],
+                in0=raw_pairs,
+                in1=cos[:, here, :].unsqueeze(3).to_broadcast([P, TILES, PAIRS, 2]),
+                op=ALU.mult,
+            )
+            nc.vector.tensor_tensor(
+                out=crossed[:, 0], in0=raw_pairs[:, :, :, 1], in1=neg_sin[:, here, :], op=ALU.mult
+            )
+            nc.vector.tensor_tensor(
+                out=crossed[:, 1], in0=raw_pairs[:, :, :, 0], in1=sin[:, here, :], op=ALU.mult
+            )
+
+            kv_cache = resident.tile([P, TILES, LATENT], F32)
+            for t in range(TILES):
+                nc.vector.scalar_tensor_tensor(
+                    out=kv_cache[:, t, :],
+                    in0=latent[:, t, :],
+                    scalar=inv_rms[:, t : t + 1],
+                    in1=gain[:],
+                    op0=ALU.mult,
+                    op1=ALU.mult,
+                )
+            nc.sync.dma_start(
+                out=out_0[b].rearrange("(p i) c -> p i c", i=PER_PARTITION)[:, here, :],
+                in_=kv_cache[:],
+            )
+
+            k_pe = resident.tile([P, TILES, PAIRS, 2], F32)
+            nc.vector.tensor_tensor(
+                out=k_pe[:], in0=direct[:], in1=crossed[:].rearrange("p e t j -> p t j e"), op=ALU.add
+            )
+            nc.sync.dma_start(
+                out=out_1[b].rearrange("(p i) c -> p i c", i=PER_PARTITION)[:, here, :],
+                in_=k_pe[:].rearrange("p t j e -> p t (j e)"),
+            )
+
+        for step in range(GROUPS + 2):
+            if step < GROUPS:
+                transpose_group(step)
+            if 1 <= step <= GROUPS:
+                project_group(step - 1)
+            if step >= 2:
+                finish_group(step - 2)

@@ -205,7 +205,7 @@ def tile_simplemla_pa_t_kernel(tc, x, wkv_a, kv_norm_w, out_0, out_1):
             )
 
             k_pe = resident.tile([P, TILES, PAIRS, 2], F32)
-            nc.vector.tensor_tensor(
+            nc.gpsimd.tensor_tensor(
                 out=k_pe[:], in0=direct[:], in1=crossed[:].rearrange("p e t j -> p t j e"), op=ALU.add
             )
             nc.sync.dma_start(

@@ -93,6 +93,7 @@ def tile_simplemla_pa_t_kernel(tc, x, wkv_a, kv_norm_w, out_0, out_1):
         work = stack.enter_context(tc.tile_pool(name="work", bufs=3))
         psum_t = stack.enter_context(tc.psum_pool(name="psum_t", bufs=4))
         psum_kv = stack.enter_context(tc.psum_pool(name="psum_kv", bufs=2))
+        stack.enter_context(tc.manual_schedule())
 
         w_rows = const.tile([P, 2 * DIM], BF16)
         nc.sync.dma_start(
@@ -160,18 +161,20 @@ def tile_simplemla_pa_t_kernel(tc, x, wkv_a, kv_norm_w, out_0, out_1):
                     func=ACT.Square,
                     accum_out=sum_squares[:, t : t + 1],
                 )
-            rms = work.tile([P, TILES], F32)
+            inv_rms = work.tile([P, TILES], F32)
             nc.scalar.activation(
-                out=rms[:], in_=sum_squares[:], func=ACT.Sqrt, scale=1.0 / LATENT, bias=EPS
+                out=inv_rms[:],
+                in_=sum_squares[:],
+                func=ACT.Abs_reciprocal_sqrt,
+                scale=1.0 / LATENT,
+                bias=EPS,
             )
-            kv_of[g] = (latent, raw, rms)
+            kv_of[g] = (latent, raw, inv_rms)
 
         def finish_group(g):
             b, half = divmod(g, HALVES)
             here = slice(half * TILES, (half + 1) * TILES)
-            latent, raw, rms = kv_of[g]
-            inv_rms = work.tile([P, TILES], F32)
-            nc.vector.reciprocal(out=inv_rms[:], in_=rms[:])
+            latent, raw, inv_rms = kv_of[g]
 
             raw_pairs = raw[:].rearrange("p t (j e) -> p t j e", e=2)
             direct = work.tile([P, TILES, PAIRS, 2], F32)
@@ -205,7 +208,7 @@ def tile_simplemla_pa_t_kernel(tc, x, wkv_a, kv_norm_w, out_0, out_1):
             )
 
             k_pe = resident.tile([P, TILES, PAIRS, 2], F32)
-            nc.gpsimd.tensor_tensor(
+            nc.vector.tensor_tensor(
                 out=k_pe[:], in0=direct[:], in1=crossed[:].rearrange("p e t j -> p t j e"), op=ALU.add
             )
             nc.sync.dma_start(

@@ -76,13 +76,12 @@ def rotation_tables(nc, const):
     )
     part = const.tile([P, 2, PER_PARTITION, PAIRS], F32)
     nc.vector.tensor_tensor(out=part[:], in0=turns[:], in1=whole[:], op=ALU.subtract)
-    sin = const.tile([P, PER_PARTITION, PAIRS], F32)
-    neg_sin = const.tile([P, PER_PARTITION, PAIRS], F32)
     cos = const.tile([P, PER_PARTITION, PAIRS], F32)
-    nc.scalar.activation(out=sin[:], in_=part[:, 0], func=ACT.Sin, scale=2.0 * math.pi)
-    nc.scalar.activation(out=neg_sin[:], in_=part[:, 0], func=ACT.Sin, scale=-2.0 * math.pi)
+    signed_sin = const.tile([P, PER_PARTITION, PAIRS, 2], F32)
+    nc.scalar.activation(out=signed_sin[:, :, :, 0], in_=part[:, 0], func=ACT.Sin, scale=-2.0 * math.pi)
+    nc.scalar.activation(out=signed_sin[:, :, :, 1], in_=part[:, 0], func=ACT.Sin, scale=2.0 * math.pi)
     nc.scalar.activation(out=cos[:], in_=part[:, 1], func=ACT.Sin, scale=2.0 * math.pi)
-    return sin, neg_sin, cos
+    return cos, signed_sin
 
 
 def tile_simplemla_pa_t_kernel(tc, x, wkv_a, kv_norm_w, out_0, out_1):
@@ -116,7 +115,7 @@ def tile_simplemla_pa_t_kernel(tc, x, wkv_a, kv_norm_w, out_0, out_1):
 
         identity = const.tile([P, P], F32)
         make_identity(nc, identity[:])
-        sin, neg_sin, cos = rotation_tables(nc, const)
+        cos, signed_sin = rotation_tables(nc, const)
 
         w_grouped = const.tile([P, 2 * DIM], BF16, align_bytes=64)
         transpose_for_quantize(nc, psum_t, identity, w_rows, w_grouped, 2)
@@ -125,6 +124,7 @@ def tile_simplemla_pa_t_kernel(tc, x, wkv_a, kv_norm_w, out_0, out_1):
         nc.vector.quantize_mx(out=w_codes[:].bitcast(FP8X4), scales=w_scales[:], in_=w_grouped[:])
 
         grouped_of = {}
+        codes_of = {}
         kv_of = {}
 
         def transpose_group(g):
@@ -132,12 +132,16 @@ def tile_simplemla_pa_t_kernel(tc, x, wkv_a, kv_norm_w, out_0, out_1):
             transpose_for_quantize(nc, psum_t, identity, x_rows[g], x_grouped, TILES)
             grouped_of[g] = x_grouped
 
-        def project_group(g):
+        def quantise_group(g):
             x_codes = work.tile([P, TILES * P], U32, align_bytes=64)
             x_scales = work.tile([P, TILES * P], U8, align_bytes=64)
             nc.vector.quantize_mx(
                 out=x_codes[:].bitcast(FP8X4), scales=x_scales[:], in_=grouped_of[g][:]
             )
+            codes_of[g] = (x_codes, x_scales)
+
+        def project_group(g):
+            x_codes, x_scales = codes_of[g]
             latent = psum_kv.tile([P, TILES, LATENT], F32)
             raw = psum_kv.tile([P, TILES, ROPE], F32)
             for t in range(TILES):
@@ -171,14 +175,18 @@ def tile_simplemla_pa_t_kernel(tc, x, wkv_a, kv_norm_w, out_0, out_1):
             )
             kv_of[g] = (latent, raw, inv_rms)
 
-        def finish_group(g):
+        def output_rows(out, g):
             b, half = divmod(g, HALVES)
-            here = slice(half * TILES, (half + 1) * TILES)
-            latent, raw, inv_rms = kv_of[g]
+            return out[b].rearrange("(p i) c -> p i c", i=PER_PARTITION)[
+                :, half * TILES : (half + 1) * TILES, :
+            ]
 
-            raw_pairs = raw[:].rearrange("p t (j e) -> p t j e", e=2)
+        def rotate_group(g):
+            half = g % HALVES
+            here = slice(half * TILES, (half + 1) * TILES)
+            raw_pairs = kv_of[g][1][:].rearrange("p t (j e) -> p t j e", e=2)
             direct = work.tile([P, TILES, PAIRS, 2], F32)
-            crossed = work.tile([P, 2, TILES, PAIRS], F32)
+            crossed = work.tile([P, TILES, PAIRS, 2], F32)
             nc.vector.tensor_tensor(
                 out=direct[:],
                 in0=raw_pairs,
@@ -186,12 +194,14 @@ def tile_simplemla_pa_t_kernel(tc, x, wkv_a, kv_norm_w, out_0, out_1):
                 op=ALU.mult,
             )
             nc.vector.tensor_tensor(
-                out=crossed[:, 0], in0=raw_pairs[:, :, :, 1], in1=neg_sin[:, here, :], op=ALU.mult
+                out=crossed[:], in0=raw_pairs[:, :, :, ::-1], in1=signed_sin[:, here, :, :], op=ALU.mult
             )
-            nc.vector.tensor_tensor(
-                out=crossed[:, 1], in0=raw_pairs[:, :, :, 0], in1=sin[:, here, :], op=ALU.mult
-            )
+            k_pe = resident.tile([P, TILES, PAIRS, 2], F32)
+            nc.gpsimd.tensor_tensor(out=k_pe[:], in0=direct[:], in1=crossed[:], op=ALU.add)
+            return k_pe
 
+        def normalise_group(g):
+            latent, raw, inv_rms = kv_of[g]
             kv_cache = resident.tile([P, TILES, LATENT], F32)
             for t in range(TILES):
                 nc.vector.scalar_tensor_tensor(
@@ -202,24 +212,21 @@ def tile_simplemla_pa_t_kernel(tc, x, wkv_a, kv_norm_w, out_0, out_1):
                     op0=ALU.mult,
                     op1=ALU.mult,
                 )
-            nc.sync.dma_start(
-                out=out_0[b].rearrange("(p i) c -> p i c", i=PER_PARTITION)[:, here, :],
-                in_=kv_cache[:],
-            )
+            return kv_cache
 
-            k_pe = resident.tile([P, TILES, PAIRS, 2], F32)
-            nc.vector.tensor_tensor(
-                out=k_pe[:], in0=direct[:], in1=crossed[:].rearrange("p e t j -> p t j e"), op=ALU.add
-            )
-            nc.sync.dma_start(
-                out=out_1[b].rearrange("(p i) c -> p i c", i=PER_PARTITION)[:, here, :],
-                in_=k_pe[:].rearrange("p t j e -> p t (j e)"),
-            )
-
-        for step in range(GROUPS + 2):
-            if step < GROUPS:
-                transpose_group(step)
-            if 1 <= step <= GROUPS:
-                project_group(step - 1)
-            if step >= 2:
-                finish_group(step - 2)
+        for g in range(-3, GROUPS):
+            ahead, far_ahead = g + 2, g + 3
+            if g >= 0:
+                k_pe = rotate_group(g)
+            if 0 <= ahead < GROUPS:
+                quantise_group(ahead)
+            if g >= 0:
+                kv_cache = normalise_group(g)
+                nc.sync.dma_start(out=output_rows(out_0, g), in_=kv_cache[:])
+                nc.sync.dma_start(
+                    out=output_rows(out_1, g), in_=k_pe[:].rearrange("p t j e -> p t (j e)")
+                )
+            if far_ahead < GROUPS:
+                transpose_group(far_ahead)
+            if 0 <= ahead < GROUPS:
+                project_group(ahead)

@@ -90,7 +90,7 @@ def tile_simplemla_pa_t_kernel(tc, x, wkv_a, kv_norm_w, out_0, out_1):
         const = stack.enter_context(tc.tile_pool(name="const", bufs=1))
         resident = stack.enter_context(tc.tile_pool(name="resident", bufs=GROUPS))
         work = stack.enter_context(tc.tile_pool(name="work", bufs=3))
-        psum_t = stack.enter_context(tc.psum_pool(name="psum_t", bufs=4))
+        psum_t = stack.enter_context(tc.psum_pool(name="psum_t", bufs=2))
         psum_kv = stack.enter_context(tc.psum_pool(name="psum_kv", bufs=2))
         stack.enter_context(tc.manual_schedule())
 
@@ -119,9 +119,23 @@ def tile_simplemla_pa_t_kernel(tc, x, wkv_a, kv_norm_w, out_0, out_1):
 
         w_grouped = const.tile([P, 2 * DIM], BF16, align_bytes=64)
         transpose_for_quantize(nc, psum_t, identity, w_rows, w_grouped, 2)
-        w_codes = const.tile([P, 2 * P], U32, align_bytes=64)
-        w_scales = const.tile([P, 2 * P], U8, align_bytes=64)
-        nc.vector.quantize_mx(out=w_codes[:].bitcast(FP8X4), scales=w_scales[:], in_=w_grouped[:])
+        w_swapped = const.tile([P, DIM], BF16, align_bytes=64)
+        nc.vector.tensor_copy(
+            out=w_swapped[:].bitcast(F32).rearrange("p (j e u) -> p j e u", e=2, u=2),
+            in_=w_grouped[:, DIM : 2 * DIM]
+            .bitcast(F32)
+            .rearrange("p (j e u) -> p j e u", e=2, u=2)[:, :, ::-1, :],
+        )
+        w_codes = const.tile([P, 3 * P], U32, align_bytes=64)
+        w_scales = const.tile([P, 3 * P], U8, align_bytes=64)
+        nc.vector.quantize_mx(
+            out=w_codes[:, 0 : 2 * P].bitcast(FP8X4), scales=w_scales[:, 0 : 2 * P], in_=w_grouped[:]
+        )
+        nc.vector.quantize_mx(
+            out=w_codes[:, 2 * P : 3 * P].bitcast(FP8X4),
+            scales=w_scales[:, 2 * P : 3 * P],
+            in_=w_swapped[:],
+        )
 
         grouped_of = {}
         codes_of = {}
@@ -144,9 +158,11 @@ def tile_simplemla_pa_t_kernel(tc, x, wkv_a, kv_norm_w, out_0, out_1):
             x_codes, x_scales = codes_of[g]
             latent = psum_kv.tile([P, TILES, LATENT], F32)
             raw = psum_kv.tile([P, TILES, ROPE], F32)
+            swapped = psum_kv.tile([P, TILES, ROPE], F32)
             for t in range(TILES):
                 tokens = slice(t * P, (t + 1) * P)
-                for result, columns in ((latent, slice(0, LATENT)), (raw, slice(LATENT, LATENT + ROPE))):
+                for w_set, result in enumerate((latent, raw, swapped)):
+                    columns = slice(w_set * P, (w_set + 1) * P)
                     nc.tensor.matmul_mx(
                         out=result[:, t, :],
                         lhsT=x_codes[:, tokens].bitcast(FP8X4),
@@ -173,7 +189,7 @@ def tile_simplemla_pa_t_kernel(tc, x, wkv_a, kv_norm_w, out_0, out_1):
                 scale=1.0 / LATENT,
                 bias=EPS,
             )
-            kv_of[g] = (latent, raw, inv_rms)
+            kv_of[g] = (latent, raw, swapped, inv_rms)
 
         def output_rows(out, g):
             b, half = divmod(g, HALVES)
@@ -184,24 +200,27 @@ def tile_simplemla_pa_t_kernel(tc, x, wkv_a, kv_norm_w, out_0, out_1):
         def rotate_group(g):
             half = g % HALVES
             here = slice(half * TILES, (half + 1) * TILES)
-            raw_pairs = kv_of[g][1][:].rearrange("p t (j e) -> p t j e", e=2)
+            latent, raw, swapped, inv_rms = kv_of[g]
             direct = work.tile([P, TILES, PAIRS, 2], F32)
             crossed = work.tile([P, TILES, PAIRS, 2], F32)
             nc.vector.tensor_tensor(
                 out=direct[:],
-                in0=raw_pairs,
+                in0=raw[:].rearrange("p t (j e) -> p t j e", e=2),
                 in1=cos[:, here, :].unsqueeze(3).to_broadcast([P, TILES, PAIRS, 2]),
                 op=ALU.mult,
             )
             nc.vector.tensor_tensor(
-                out=crossed[:], in0=raw_pairs[:, :, :, ::-1], in1=signed_sin[:, here, :, :], op=ALU.mult
+                out=crossed[:],
+                in0=swapped[:].rearrange("p t (j e) -> p t j e", e=2),
+                in1=signed_sin[:, here, :, :],
+                op=ALU.mult,
             )
             k_pe = resident.tile([P, TILES, PAIRS, 2], F32)
             nc.gpsimd.tensor_tensor(out=k_pe[:], in0=direct[:], in1=crossed[:], op=ALU.add)
             return k_pe
 
         def normalise_group(g):
-            latent, raw, inv_rms = kv_of[g]
+            latent, raw, swapped, inv_rms = kv_of[g]
             kv_cache = resident.tile([P, TILES, LATENT], F32)
             for t in range(TILES):
                 nc.vector.scalar_tensor_tensor(

@@ -26,6 +26,7 @@ PER_PARTITION = SEQ // P
 TILES = 4
 HALVES = PER_PARTITION // TILES
 GROUPS = BATCH * HALVES
+GPSIMD_TILES = 3
 
 ROUND = 1.5 * 2.0**23
 
@@ -90,7 +91,7 @@ def tile_simplemla_pa_t_kernel(tc, x, wkv_a, kv_norm_w, out_0, out_1):
         const = stack.enter_context(tc.tile_pool(name="const", bufs=1))
         resident = stack.enter_context(tc.tile_pool(name="resident", bufs=GROUPS))
         work = stack.enter_context(tc.tile_pool(name="work", bufs=3))
-        psum_t = stack.enter_context(tc.psum_pool(name="psum_t", bufs=2))
+        psum_t = stack.enter_context(tc.psum_pool(name="psum_t", bufs=4))
         psum_kv = stack.enter_context(tc.psum_pool(name="psum_kv", bufs=2))
         stack.enter_context(tc.manual_schedule())
 
@@ -119,23 +120,9 @@ def tile_simplemla_pa_t_kernel(tc, x, wkv_a, kv_norm_w, out_0, out_1):
 
         w_grouped = const.tile([P, 2 * DIM], BF16, align_bytes=64)
         transpose_for_quantize(nc, psum_t, identity, w_rows, w_grouped, 2)
-        w_swapped = const.tile([P, DIM], BF16, align_bytes=64)
-        nc.vector.tensor_copy(
-            out=w_swapped[:].bitcast(F32).rearrange("p (j e u) -> p j e u", e=2, u=2),
-            in_=w_grouped[:, DIM : 2 * DIM]
-            .bitcast(F32)
-            .rearrange("p (j e u) -> p j e u", e=2, u=2)[:, :, ::-1, :],
-        )
-        w_codes = const.tile([P, 3 * P], U32, align_bytes=64)
-        w_scales = const.tile([P, 3 * P], U8, align_bytes=64)
-        nc.vector.quantize_mx(
-            out=w_codes[:, 0 : 2 * P].bitcast(FP8X4), scales=w_scales[:, 0 : 2 * P], in_=w_grouped[:]
-        )
-        nc.vector.quantize_mx(
-            out=w_codes[:, 2 * P : 3 * P].bitcast(FP8X4),
-            scales=w_scales[:, 2 * P : 3 * P],
-            in_=w_swapped[:],
-        )
+        w_codes = const.tile([P, 2 * P], U32, align_bytes=64)
+        w_scales = const.tile([P, 2 * P], U8, align_bytes=64)
+        nc.vector.quantize_mx(out=w_codes[:].bitcast(FP8X4), scales=w_scales[:], in_=w_grouped[:])
 
         grouped_of = {}
         codes_of = {}
@@ -158,11 +145,9 @@ def tile_simplemla_pa_t_kernel(tc, x, wkv_a, kv_norm_w, out_0, out_1):
             x_codes, x_scales = codes_of[g]
             latent = psum_kv.tile([P, TILES, LATENT], F32)
             raw = psum_kv.tile([P, TILES, ROPE], F32)
-            swapped = psum_kv.tile([P, TILES, ROPE], F32)
             for t in range(TILES):
                 tokens = slice(t * P, (t + 1) * P)
-                for w_set, result in enumerate((latent, raw, swapped)):
-                    columns = slice(w_set * P, (w_set + 1) * P)
+                for result, columns in ((latent, slice(0, LATENT)), (raw, slice(LATENT, LATENT + ROPE))):
                     nc.tensor.matmul_mx(
                         out=result[:, t, :],
                         lhsT=x_codes[:, tokens].bitcast(FP8X4),
@@ -189,7 +174,7 @@ def tile_simplemla_pa_t_kernel(tc, x, wkv_a, kv_norm_w, out_0, out_1):
                 scale=1.0 / LATENT,
                 bias=EPS,
             )
-            kv_of[g] = (latent, raw, swapped, inv_rms)
+            kv_of[g] = (latent, raw, inv_rms)
 
         def output_rows(out, g):
             b, half = divmod(g, HALVES)
@@ -200,27 +185,37 @@ def tile_simplemla_pa_t_kernel(tc, x, wkv_a, kv_norm_w, out_0, out_1):
         def rotate_group(g):
             half = g % HALVES
             here = slice(half * TILES, (half + 1) * TILES)
-            latent, raw, swapped, inv_rms = kv_of[g]
+            raw_pairs = kv_of[g][1][:].rearrange("p t (j e) -> p t j e", e=2)
             direct = work.tile([P, TILES, PAIRS, 2], F32)
             crossed = work.tile([P, TILES, PAIRS, 2], F32)
             nc.vector.tensor_tensor(
                 out=direct[:],
-                in0=raw[:].rearrange("p t (j e) -> p t j e", e=2),
+                in0=raw_pairs,
                 in1=cos[:, here, :].unsqueeze(3).to_broadcast([P, TILES, PAIRS, 2]),
                 op=ALU.mult,
             )
             nc.vector.tensor_tensor(
-                out=crossed[:],
-                in0=swapped[:].rearrange("p t (j e) -> p t j e", e=2),
-                in1=signed_sin[:, here, :, :],
-                op=ALU.mult,
+                out=crossed[:], in0=raw_pairs[:, :, :, ::-1], in1=signed_sin[:, here, :, :], op=ALU.mult
             )
             k_pe = resident.tile([P, TILES, PAIRS, 2], F32)
-            nc.gpsimd.tensor_tensor(out=k_pe[:], in0=direct[:], in1=crossed[:], op=ALU.add)
-            return k_pe
+            nc.gpsimd.tensor_tensor(
+                out=k_pe[:, 0:GPSIMD_TILES],
+                in0=direct[:, 0:GPSIMD_TILES],
+                in1=crossed[:, 0:GPSIMD_TILES],
+                op=ALU.add,
+            )
+            return direct, crossed, k_pe
+
+        def finish_rotation(direct, crossed, k_pe):
+            nc.vector.tensor_tensor(
+                out=k_pe[:, GPSIMD_TILES:TILES],
+                in0=direct[:, GPSIMD_TILES:TILES],
+                in1=crossed[:, GPSIMD_TILES:TILES],
+                op=ALU.add,
+            )
 
         def normalise_group(g):
-            latent, raw, swapped, inv_rms = kv_of[g]
+            latent, raw, inv_rms = kv_of[g]
             kv_cache = resident.tile([P, TILES, LATENT], F32)
             for t in range(TILES):
                 nc.vector.scalar_tensor_tensor(
@@ -236,10 +231,11 @@ def tile_simplemla_pa_t_kernel(tc, x, wkv_a, kv_norm_w, out_0, out_1):
         for g in range(-3, GROUPS):
             ahead, far_ahead = g + 2, g + 3
             if g >= 0:
-                k_pe = rotate_group(g)
+                direct, crossed, k_pe = rotate_group(g)
             if 0 <= ahead < GROUPS:
                 quantise_group(ahead)
             if g >= 0:
+                finish_rotation(direct, crossed, k_pe)
                 kv_cache = normalise_group(g)
                 nc.sync.dma_start(out=output_rows(out_0, g), in_=kv_cache[:])
                 nc.sync.dma_start(

import math
from contextlib import ExitStack

import concourse.mybir as mybir
from concourse.masks import make_identity

F32 = mybir.dt.float32
BF16 = mybir.dt.bfloat16
U32 = mybir.dt.uint32
U8 = mybir.dt.uint8
FP8X4 = mybir.dt.float8_e4m3fn_x4
ALU = mybir.AluOpType
ACT = mybir.ActivationFunctionType

P = 128
BATCH, SEQ, DIM = 8, 1024, 512
LATENT, ROPE = 128, 128
PAIRS = ROPE // 2
DOUBLINGS = 6
assert 2**DOUBLINGS == PAIRS
THETA = 10000.0
EPS = 1e-6

WORDS = DIM // 2
PER_PARTITION = SEQ // P
TILES = 4
HALVES = PER_PARTITION // TILES
GROUPS = BATCH * HALVES
GPSIMD_TILES = 3

ROUND = 1.5 * 2.0**23

FLOPS = 2 * BATCH * SEQ * DIM * (LATENT + ROPE)


def transpose_for_quantize(nc, psum_t, identity, rows, grouped, row_tiles):
    row_words = rows[:].bitcast(F32)
    grouped_words = grouped[:].bitcast(F32)
    for pair in range(row_tiles // 2):
        flipped = psum_t.tile([P, 2, 2, P], F32)
        for t in range(2):
            for u in range(2):
                first = (2 * pair + t) * WORDS + u * P
                nc.tensor.transpose(flipped[:, t, u, :], row_words[:, first : first + P], identity[:])
        nc.scalar.copy(
            out=grouped_words[:, 2 * pair * WORDS : 2 * (pair + 1) * WORDS].rearrange(
                "p (t r u) -> p t r u", t=2, u=2
            ),
            in_=flipped[:].rearrange("p t u r -> p t r u"),
        )


def rotation_tables(nc, const):
    position = const.tile([P, PER_PARTITION], F32)
    nc.gpsimd.iota(
        position[:],
        pattern=[[1, PER_PARTITION]],
        base=0,
        channel_multiplier=PER_PARTITION,
        allow_small_or_imprecise_dtypes=True,
    )
    turns = const.tile([P, 2, PER_PARTITION, PAIRS], F32)
    nc.vector.tensor_scalar_mul(
        out=turns[:, 0, :, 0:1], in0=position[:].unsqueeze(2), scalar1=1.0 / (2.0 * math.pi)
    )
    for doubling in range(DOUBLINGS):
        width = 2**doubling
        nc.vector.tensor_scalar_mul(
            out=turns[:, 0, :, width : 2 * width],
            in0=turns[:, 0, :, 0:width],
            scalar1=THETA ** (-2.0 * width / ROPE),
        )
    nc.vector.tensor_scalar_add(out=turns[:, 1], in0=turns[:, 0], scalar1=0.25)
    whole = const.tile([P, 2, PER_PARTITION, PAIRS], F32)
    nc.vector.tensor_scalar(
        out=whole[:], in0=turns[:], scalar1=ROUND, scalar2=ROUND, op0=ALU.add, op1=ALU.subtract
    )
    part = const.tile([P, 2, PER_PARTITION, PAIRS], F32)
    nc.vector.tensor_tensor(out=part[:], in0=turns[:], in1=whole[:], op=ALU.subtract)
    cos = const.tile([P, PER_PARTITION, PAIRS], F32)
    signed_sin = const.tile([P, PER_PARTITION, PAIRS, 2], F32)
    nc.scalar.activation(out=signed_sin[:, :, :, 0], in_=part[:, 0], func=ACT.Sin, scale=-2.0 * math.pi)
    nc.scalar.activation(out=signed_sin[:, :, :, 1], in_=part[:, 0], func=ACT.Sin, scale=2.0 * math.pi)
    nc.scalar.activation(out=cos[:], in_=part[:, 1], func=ACT.Sin, scale=2.0 * math.pi)
    return cos, signed_sin


def tile_simplemla_pa_t_kernel(tc, x, wkv_a, kv_norm_w, out_0, out_1):
    nc = tc.nc
    with ExitStack() as stack:
        const = stack.enter_context(tc.tile_pool(name="const", bufs=1))
        resident = stack.enter_context(tc.tile_pool(name="resident", bufs=GROUPS))
        work = stack.enter_context(tc.tile_pool(name="work", bufs=3))
        psum_t = stack.enter_context(tc.psum_pool(name="psum_t", bufs=4))
        psum_kv = stack.enter_context(tc.psum_pool(name="psum_kv", bufs=2))
        stack.enter_context(tc.manual_schedule())

        w_rows = const.tile([P, 2 * DIM], BF16)
        nc.sync.dma_start(
            out=w_rows[:].rearrange("p (a k) -> p a k", a=2),
            in_=wkv_a.rearrange("(a p) k -> p a k", p=P),
        )
        gain = const.tile([P, LATENT], BF16)
        nc.scalar.dma_start(out=gain[:], in_=kv_norm_w.partition_broadcast(P))
        x_rows = []
        for g in range(GROUPS):
            b, half = divmod(g, HALVES)
            x_group = resident.tile([P, TILES * DIM], BF16)
            nc.sync.dma_start(
                out=x_group[:].rearrange("p (i k) -> p i k", i=TILES),
                in_=x[b].rearrange("(p i) k -> p i k", i=PER_PARTITION)[
                    :, half * TILES : (half + 1) * TILES, :
                ],
            )
            x_rows.append(x_group)

        identity = const.tile([P, P], F32)
        make_identity(nc, identity[:])
        cos, signed_sin = rotation_tables(nc, const)

        w_grouped = const.tile([P, 2 * DIM], BF16, align_bytes=64)
        transpose_for_quantize(nc, psum_t, identity, w_rows, w_grouped, 2)
        w_codes = const.tile([P, 2 * P], U32, align_bytes=64)
        w_scales = const.tile([P, 2 * P], U8, align_bytes=64)
        nc.vector.quantize_mx(out=w_codes[:].bitcast(FP8X4), scales=w_scales[:], in_=w_grouped[:])

        grouped_of = {}
        codes_of = {}
        kv_of = {}

        def transpose_group(g):
            x_grouped = work.tile([P, TILES * DIM], BF16, align_bytes=64)
            transpose_for_quantize(nc, psum_t, identity, x_rows[g], x_grouped, TILES)
            grouped_of[g] = x_grouped

        def quantise_group(g):
            x_codes = work.tile([P, TILES * P], U32, align_bytes=64)
            x_scales = work.tile([P, TILES * P], U8, align_bytes=64)
            nc.vector.quantize_mx(
                out=x_codes[:].bitcast(FP8X4), scales=x_scales[:], in_=grouped_of[g][:]
            )
            codes_of[g] = (x_codes, x_scales)

        def project_group(g):
            x_codes, x_scales = codes_of[g]
            latent = psum_kv.tile([P, TILES, LATENT], F32)
            raw = psum_kv.tile([P, TILES, ROPE], F32)
            for t in range(TILES):
                tokens = slice(t * P, (t + 1) * P)
                for result, columns in ((latent, slice(0, LATENT)), (raw, slice(LATENT, LATENT + ROPE))):
                    nc.tensor.matmul_mx(
                        out=result[:, t, :],
                        lhsT=x_codes[:, tokens].bitcast(FP8X4),
                        lhsT_scale=x_scales[:, tokens],
                        rhs=w_codes[:, columns].bitcast(FP8X4),
                        rhs_scale=w_scales[:, columns],
                        start=True,
                        stop=True,
                    )
            squares = work.tile([P, TILES, LATENT], F32)
            sum_squares = work.tile([P, TILES], F32)
            for t in range(TILES):
                nc.scalar.activation(
                    out=squares[:, t, :],
                    in_=latent[:, t, :],
                    func=ACT.Square,
                    accum_out=sum_squares[:, t : t + 1],
                )
            inv_rms = work.tile([P, TILES], F32)
            nc.scalar.activation(
                out=inv_rms[:],
                in_=sum_squares[:],
                func=ACT.Abs_reciprocal_sqrt,
                scale=1.0 / LATENT,
                bias=EPS,
            )
            kv_of[g] = (latent, raw, inv_rms)

        def output_rows(out, g):
            b, half = divmod(g, HALVES)
            return out[b].rearrange("(p i) c -> p i c", i=PER_PARTITION)[
                :, half * TILES : (half + 1) * TILES, :
            ]

        def rotate_group(g):
            half = g % HALVES
            here = slice(half * TILES, (half + 1) * TILES)
            raw_pairs = kv_of[g][1][:].rearrange("p t (j e) -> p t j e", e=2)
            direct = work.tile([P, TILES, PAIRS, 2], F32)
            crossed = work.tile([P, TILES, PAIRS, 2], F32)
            nc.vector.tensor_tensor(
                out=direct[:],
                in0=raw_pairs,
                in1=cos[:, here, :].unsqueeze(3).to_broadcast([P, TILES, PAIRS, 2]),
                op=ALU.mult,
            )
            nc.vector.tensor_tensor(
                out=crossed[:], in0=raw_pairs[:, :, :, ::-1], in1=signed_sin[:, here, :, :], op=ALU.mult
            )
            k_pe = resident.tile([P, TILES, PAIRS, 2], F32)
            nc.gpsimd.tensor_tensor(
                out=k_pe[:, 0:GPSIMD_TILES],
                in0=direct[:, 0:GPSIMD_TILES],
                in1=crossed[:, 0:GPSIMD_TILES],
                op=ALU.add,
            )
            return direct, crossed, k_pe

        def finish_rotation(direct, crossed, k_pe):
            nc.vector.tensor_tensor(
                out=k_pe[:, GPSIMD_TILES:TILES],
                in0=direct[:, GPSIMD_TILES:TILES],
                in1=crossed[:, GPSIMD_TILES:TILES],
                op=ALU.add,
            )

        def normalise_group(g):
            latent, raw, inv_rms = kv_of[g]
            kv_cache = resident.tile([P, TILES, LATENT], F32)
            for t in range(TILES):
                nc.vector.scalar_tensor_tensor(
                    out=kv_cache[:, t, :],
                    in0=latent[:, t, :],
                    scalar=inv_rms[:, t : t + 1],
                    in1=gain[:],
                    op0=ALU.mult,
                    op1=ALU.mult,
                )
            return kv_cache

        for g in range(-3, GROUPS):
            ahead, far_ahead = g + 2, g + 3
            if g >= 0:
                direct, crossed, k_pe = rotate_group(g)
            if 0 <= ahead < GROUPS:
                quantise_group(ahead)
            if g >= 0:
                finish_rotation(direct, crossed, k_pe)
                kv_cache = normalise_group(g)
                nc.sync.dma_start(out=output_rows(out_0, g), in_=kv_cache[:])
                nc.sync.dma_start(
                    out=output_rows(out_1, g), in_=k_pe[:].rearrange("p t j e -> p t (j e)")
                )
            if far_ahead < GROUPS:
                transpose_group(far_ahead)
            if 0 <= ahead < GROUPS:
                project_group(ahead)
